import numpy as np
import ml_dtypes


def mxq(x, axis, fmt="e4m3"):
    dtype, down = {"e4m3": (ml_dtypes.float8_e4m3fn, 7), "e5m2": (ml_dtypes.float8_e5m2, 14)}[fmt]
    v = np.moveaxis(np.asarray(x, np.float32).astype(ml_dtypes.bfloat16).astype(np.float64), axis, -1)
    blocks = v.reshape(v.shape[:-1] + (-1, 32))
    amax = np.abs(blocks).max(-1, keepdims=True)
    byte = np.maximum(np.where(amax > 0, np.frexp(amax)[1] - 1 + 127, 0) - down, 1)
    scale = np.exp2(byte - 127.0)
    codes = (blocks / scale).astype(np.float32).astype(dtype).astype(np.float64)
    return np.moveaxis((codes * scale).reshape(v.shape), -1, axis)


WIDE = False


def mx_kscale(k):
    if not WIDE:
        return np.ones(k)
    levels = np.array([10, -10, 5, -5, 0])
    a = np.random.permutation(np.resize(levels, k // 512 * 4)).reshape(k // 512, 4)
    idx = np.arange(k)
    return np.exp2(a[idx // 512, idx % 128 // 32])


BF16 = ml_dtypes.bfloat16


def bf(x):
    return np.asarray(x, np.float32).astype(BF16)


def f64(x):
    return np.asarray(x).astype(np.float64)


B, S, D, E, F = 4, 1024, 512, 1024, 256
EPS = 1e-5


def layernorm(x, g, b):
    m = x.mean(-1, keepdims=True)
    v = ((x - m) ** 2).mean(-1, keepdims=True)
    return (x - m) * (1.0 / np.sqrt(v + EPS)) * g + b


def setup_inputs():
    s, t = mx_kscale(E), mx_kscale(D)
    return {"attn": bf(0.4 * np.random.standard_normal((B, S, E)) * s),
            "src_norm": bf(np.random.standard_normal((B, S, D)) + 0.3),
            "Wo": bf(np.random.standard_normal((D, E)) / np.sqrt(E) / s[None, :]),
            "bo": bf(0.1 * np.random.standard_normal(D)),
            "g2": bf((1.0 + 0.1 * np.random.standard_normal(D)) * t),
            "be2": bf(0.1 * np.random.standard_normal(D) * t),
            "W1": bf(np.random.standard_normal((F, D)) / np.sqrt(D) / t[None, :]),
            "b1": bf(0.1 * np.random.standard_normal(F))}


def reference(attn, src_norm, Wo, bo, g2, be2, W1, b1):
    x = f64(src_norm) + (mxq(f64(attn), 2, "e4m3") @ mxq(f64(Wo), 1, "e4m3").T) + f64(bo)
    h = layernorm(x, f64(g2), f64(be2))
    u = np.maximum((mxq(h, 2, "e4m3") @ mxq(f64(W1), 1, "e4m3").T) + f64(b1), 0.0)
    return x, u

@@ -1,0 +1,336 @@
+from contextlib import ExitStack
+
+import concourse.mybir as mybir
+from concourse.masks import make_identity
+
+F32 = mybir.dt.float32
+BF16 = mybir.dt.bfloat16
+U32 = mybir.dt.uint32
+U8 = mybir.dt.uint8
+FP8X4 = mybir.dt.float8_e4m3fn_x4
+ALU = mybir.AluOpType
+ACT = mybir.ActivationFunctionType
+
+P = 128
+PACK = 4
+K_PASS = P * PACK
+TOKENS, E, D, F = 4096, 1024, 512, 256
+EPS = 1e-5
+E_PASSES = E // K_PASS
+J = 2
+GROUP = J * P
+N_GROUPS = TOKENS // GROUP
+LOAD_AHEAD = 5
+FLOPS = 2 * TOKENS * (E * D + D * F)
+
+
+def transpose_blocks(nc, bank, rows, ident):
+    for b in range(PACK):
+        nc.tensor.transpose(bank[:, b, :], rows[:, b * P : (b + 1) * P], ident)
+
+
+def words_side_by_side(bank):
+    return bank.rearrange("p (g u) c -> p g c u", u=2)
+
+
+def tile_rotaryembeddingtransformerlayer_pb_t_kernel(
+    tc, attn, src_norm, Wo, bo, g2, be2, W1, b1, out_0, out_1
+):
+    nc = tc.nc
+    attn_groups = attn.flatten_outer_dims().rearrange("(n p j) k -> n p j k", p=P, j=J)
+    src_groups = src_norm.flatten_outer_dims().rearrange("(n p j) d -> n p j d", p=P, j=J)
+    x_groups = out_0.flatten_outer_dims().rearrange("(n p j) d -> n p j d", p=P, j=J)
+    u_groups = out_1.flatten_outer_dims().rearrange("(n p j) f -> n p j f", p=P, j=J)
+
+    with ExitStack() as ctx:
+        ctx.enter_context(tc.manual_schedule())
+        const = ctx.enter_context(tc.tile_pool(name="const", bufs=1))
+        loads = ctx.enter_context(tc.tile_pool(name="loads", bufs=LOAD_AHEAD))
+        work = ctx.enter_context(tc.tile_pool(name="work", bufs=2))
+        outs = ctx.enter_context(tc.tile_pool(name="outs", bufs=3))
+        stats = ctx.enter_context(tc.tile_pool(name="stats", bufs=3))
+        psum = ctx.enter_context(tc.psum_pool(name="psum", bufs=2))
+
+        ident = const.tile([P, P], F32)
+        make_identity(nc, ident[:])
+        eps_col = const.tile([P, 1], F32)
+        nc.vector.memset(eps_col[:], EPS)
+        table_warm = const.tile([P, 1], F32)
+        nc.scalar.activation(out=table_warm[:], in_=eps_col[:], func=ACT.Sqrt)
+
+        bias_rows = const.tile([P, D + F], BF16)
+        nc.vector.memset(bias_rows[:], 0.0)
+        nc.scalar.dma_start(out=bias_rows[0:1, 0:D], in_=bo.rearrange("(o d) -> o d", o=1))
+        nc.scalar.dma_start(out=bias_rows[0:1, D : D + F], in_=b1.rearrange("(o f) -> o f", o=1))
+        ones = const.tile([P, P], BF16)
+        nc.vector.memset(ones[:], 1.0)
+        norm_rows = const.tile([P, P], BF16)
+        nc.vector.memset(norm_rows[:], 0.0)
+        nc.scalar.dma_start(out=norm_rows[0:PACK, :], in_=g2.rearrange("(t p) -> t p", p=P))
+        nc.scalar.dma_start(out=norm_rows[PACK : 2 * PACK, :], in_=be2.rearrange("(t p) -> t p", p=P))
+        w1_rows = const.tile([P, F // P, D], BF16)
+        nc.scalar.dma_start(out=w1_rows[:], in_=W1.rearrange("(c p) d -> p c d", p=P))
+        wo_rows = const.tile([P, D // P, E], BF16)
+        wo_chunks = Wo.rearrange("(c p) k -> c p k", p=P)
+        for c in range(D // P):
+            nc.sync.dma_start(out=wo_rows[:, c, :], in_=wo_chunks[c])
+
+        bo_bank = psum.tile([P, D], F32, tag="mm1")
+        nc.tensor.matmul(out=bo_bank[:], lhsT=ones[:], rhs=bias_rows[:, 0:D], start=True, stop=True)
+        bo_all = const.tile([P, D], F32)
+        nc.vector.tensor_copy(out=bo_all[:], in_=bo_bank[:])
+        b1_bank = psum.tile([P, F], F32, tag="mm2")
+        nc.tensor.matmul(out=b1_bank[:], lhsT=ones[:], rhs=bias_rows[:, D : D + F], start=True, stop=True)
+        b1_all = const.tile([P, F], F32)
+        nc.vector.tensor_copy(out=b1_all[:], in_=b1_bank[:])
+
+        norm_rows_f32 = const.tile([P, P], F32)
+        nc.vector.tensor_copy(out=norm_rows_f32[:], in_=norm_rows[:])
+        norm_bank = psum.tile([P, P], F32, tag="z_t")
+        nc.tensor.transpose(norm_bank[:], norm_rows_f32[:], ident[:])
+        gain_shift = const.tile([P, 2 * PACK], F32)
+        nc.vector.tensor_copy(out=gain_shift[:], in_=norm_bank[:, 0 : 2 * PACK])
+
+        wo_words = wo_rows[:].bitcast(F32)
+        wo_grouped = const.tile([P, E_PASSES, D, PACK], BF16, align_bytes=64)
+        wo_grouped_words = wo_grouped[:].bitcast(F32)
+        wo_codes = const.tile([P, E_PASSES, D], U32, align_bytes=64)
+        wo_scales = const.tile([P, E_PASSES, D], U8, align_bytes=64)
+        for c in range(D // P):
+            wo_bank = psum.tile([P, PACK, P], F32, tag="attn_t")
+            transpose_blocks(nc, wo_bank, wo_words[:, c, :], ident[:])
+            copy_out = nc.vector.tensor_copy if c % 2 == 0 else nc.scalar.copy
+            copy_out(out=wo_grouped_words[:, :, c * P : (c + 1) * P, :], in_=words_side_by_side(wo_bank[:]))
+        for g in range(E_PASSES):
+            nc.vector.quantize_mx(
+                out=wo_codes[:, g, :].bitcast(FP8X4),
+                scales=wo_scales[:, g, :],
+                in_=wo_grouped[:, g, :, :].rearrange("p d t -> p (d t)"),
+            )
+
+        w1_f32 = const.tile([P, F // P, D], F32)
+        nc.vector.tensor_copy(out=w1_f32[:], in_=w1_rows[:])
+        w1_grouped = const.tile([P, F, PACK], BF16, align_bytes=64)
+        w1_codes = const.tile([P, F], U32, align_bytes=64)
+        w1_scales = const.tile([P, F], U8, align_bytes=64)
+        for c in range(F // P):
+            w1_bank = psum.tile([P, PACK, P], F32, tag="z_t")
+            transpose_blocks(nc, w1_bank, w1_f32[:, c, :], ident[:])
+            nc.vector.tensor_copy(
+                out=w1_grouped[:, c * P : (c + 1) * P, :], in_=w1_bank[:].rearrange("p t f -> p f t")
+            )
+        nc.vector.quantize_mx(
+            out=w1_codes[:].bitcast(FP8X4),
+            scales=w1_scales[:],
+            in_=w1_grouped[:].rearrange("p f t -> p (f t)"),
+        )
+
+        attn_sb, src_sb, attn_banks, attn_grouped, attn_mx = {}, {}, {}, {}, {}
+        x_sb, x_banks, neg_mean, std, inv_std, shift_z = {}, {}, {}, {}, {}, {}
+        z_sb, z_banks, h_planes, h_grouped, h_mx, u_banks = {}, {}, {}, {}, {}, {}
+
+        def load(n):
+            attn_tile = loads.tile([P, J, E], BF16)
+            nc.sync.dma_start(out=attn_tile[:], in_=attn_groups[n])
+            src_tile = loads.tile([P, J, D], BF16)
+            nc.sync.dma_start(out=src_tile[:], in_=src_groups[n])
+            attn_sb[n], src_sb[n] = attn_tile, src_tile
+
+        def transpose_attn(n):
+            attn_words = attn_sb[n][:].bitcast(F32)
+            attn_banks[n] = []
+            for j in range(J):
+                attn_bank = psum.tile([P, PACK, P], F32, tag="attn_t")
+                transpose_blocks(nc, attn_bank, attn_words[:, j, :], ident[:])
+                attn_banks[n].append(attn_bank)
+
+        def copy_attn(n):
+            attn_side = work.tile([P, J, E_PASSES, P, PACK], BF16, align_bytes=64)
+            attn_side_words = attn_side[:].bitcast(F32)
+            for j in range(J):
+                nc.scalar.copy(out=attn_side_words[:, j, :, :, :], in_=words_side_by_side(attn_banks[n][j][:]))
+            attn_grouped[n] = attn_side
+
+        def quantise_attn(n):
+            attn_codes = work.tile([P, J, E_PASSES, P], U32, align_bytes=64)
+            attn_scales = work.tile([P, J, E_PASSES, P], U8, align_bytes=64)
+            nc.vector.quantize_mx(
+                out=attn_codes[:].rearrange("p j g k -> p (j g k)").bitcast(FP8X4),
+                scales=attn_scales[:].rearrange("p j g k -> p (j g k)"),
+                in_=attn_grouped[n][:].rearrange("p j g k t -> p (j g k t)"),
+            )
+            attn_mx[n] = (attn_codes, attn_scales)
+
+        def residual(n):
+            x_tile = outs.tile([P, J, D], F32)
+            nc.vector.tensor_tensor(
+                out=x_tile[:], in0=src_sb[n][:], in1=bo_all[:].unsqueeze(1).to_broadcast([P, J, D]), op=ALU.add
+            )
+            x_sb[n] = x_tile
+
+        def first_product(n):
+            codes, scales = attn_mx[n]
+            x_banks[n] = []
+            for j in range(J):
+                x_bank = psum.tile([P, D], F32, tag="mm1")
+                for g in range(E_PASSES):
+                    nc.tensor.matmul_mx(
+                        out=x_bank[:],
+                        lhsT=codes[:, j, g, :].bitcast(FP8X4),
+                        lhsT_scale=scales[:, j, g, :],
+                        rhs=wo_codes[:, g, :].bitcast(FP8X4),
+                        rhs_scale=wo_scales[:, g, :],
+                        start=(g == 0),
+                        stop=(g == E_PASSES - 1),
+                    )
+                x_banks[n].append(x_bank)
+
+        def finish_x(n):
+            row_sum = stats.tile([P, J], F32)
+            for j in range(J):
+                nc.vector.scalar_tensor_tensor(
+                    out=x_sb[n][:, j, :],
+                    in0=x_banks[n][j][:],
+                    scalar=0.0,
+                    in1=x_sb[n][:, j, :],
+                    op0=ALU.add,
+                    op1=ALU.add,
+                    accum_out=row_sum[:, j : j + 1],
+                )
+            minus_mean = stats.tile([P, J], F32)
+            nc.vector.tensor_scalar_mul(out=minus_mean[:], in0=row_sum[:], scalar1=-1.0 / D)
+            neg_mean[n] = minus_mean
+            nc.sync.dma_start(out=x_groups[n], in_=x_sb[n][:])
+
+        def deviation(n):
+            squares = work.tile([P, J, D], BF16)
+            sum_sq = stats.tile([P, J], F32)
+            for j in range(J):
+                nc.scalar.activation(
+                    out=squares[:, j, :],
+                    in_=x_sb[n][:, j, :],
+                    func=ACT.Square,
+                    bias=neg_mean[n][:, j : j + 1],
+                    accum_out=sum_sq[:, j : j + 1],
+                )
+            std_tile = stats.tile([P, J], F32)
+            nc.scalar.activation(out=std_tile[:], in_=sum_sq[:], func=ACT.Sqrt, scale=1.0 / D, bias=eps_col[:])
+            std[n] = std_tile
+
+        def invert_std(n):
+            inv_tile = stats.tile([P, J], F32)
+            nc.vector.reciprocal(out=inv_tile[:], in_=std[n][:])
+            shift_tile = stats.tile([P, J], F32)
+            nc.vector.tensor_tensor(out=shift_tile[:], in0=neg_mean[n][:], in1=inv_tile[:], op=ALU.mult)
+            inv_std[n], shift_z[n] = inv_tile, shift_tile
+
+        def normalise(n):
+            z_tile = work.tile([P, J, D], F32)
+            for j in range(J):
+                nc.scalar.activation(
+                    out=z_tile[:, j, :],
+                    in_=x_sb[n][:, j, :],
+                    func=ACT.Identity,
+                    scale=inv_std[n][:, j : j + 1],
+                    bias=shift_z[n][:, j : j + 1],
+                )
+            z_sb[n] = z_tile
+
+        def transpose_z(n):
+            z_banks[n] = []
+            for half in range(PACK // 2):
+                z_bank = psum.tile([P, 2, GROUP], F32, tag="z_t")
+                z_banks[n].append(z_bank)
+            for j in range(J):
+                for t in range(PACK):
+                    nc.tensor.transpose(
+                        z_banks[n][t // 2][:, t % 2, j * P : (j + 1) * P],
+                        z_sb[n][:, j, t * P : (t + 1) * P],
+                        ident[:],
+                    )
+
+        def gain_and_shift(n):
+            planes = work.tile([P, PACK, GROUP], BF16)
+            for t in range(PACK):
+                nc.scalar.activation(
+                    out=planes[:, t, :],
+                    in_=z_banks[n][t // 2][:, t % 2, :],
+                    func=ACT.Identity,
+                    scale=gain_shift[:, t : t + 1],
+                    bias=gain_shift[:, PACK + t : PACK + t + 1],
+                )
+            h_planes[n] = planes
+
+        def regroup_h(n):
+            h_side = work.tile([P, GROUP, PACK], BF16, align_bytes=64)
+            nc.vector.tensor_copy(
+                out=h_side[:].rearrange("p (c i) t -> p c t i", i=4),
+                in_=h_planes[n][:].rearrange("p t (c i) -> p c t i", i=4),
+            )
+            h_grouped[n] = h_side
+
+        def quantise_h(n):
+            h_codes = work.tile([P, GROUP], U32, align_bytes=64)
+            h_scales = work.tile([P, GROUP], U8, align_bytes=64)
+            nc.vector.quantize_mx(
+                out=h_codes[:].bitcast(FP8X4), scales=h_scales[:], in_=h_grouped[n][:].rearrange("p k t -> p (k t)")
+            )
+            h_mx[n] = (h_codes, h_scales)
+
+        def second_product(n):
+            codes, scales = h_mx[n]
+            u_bank = psum.tile([P, J, F], F32, tag="mm2")
+            for j in range(J):
+                nc.tensor.matmul_mx(
+                    out=u_bank[:, j, :],
+                    lhsT=codes[:, j * P : (j + 1) * P].bitcast(FP8X4),
+                    lhsT_scale=scales[:, j * P : (j + 1) * P],
+                    rhs=w1_codes[:].bitcast(FP8X4),
+                    rhs_scale=w1_scales[:],
+                    start=True,
+                    stop=True,
+                )
+            u_banks[n] = u_bank
+
+        def finish_u(n):
+            u_tile = outs.tile([P, J, F], F32)
+            nc.vector.tensor_tensor(
+                out=u_tile[:], in0=u_banks[n][:], in1=b1_all[:].unsqueeze(1).to_broadcast([P, J, F]), op=ALU.add
+            )
+            nc.vector.tensor_scalar_max(out=u_tile[:], in0=u_tile[:], scalar1=0.0)
+            nc.sync.dma_start(out=u_groups[n], in_=u_tile[:])
+
+        def exists(n):
+            return 0 <= n < N_GROUPS
+
+        for r in range(-LOAD_AHEAD, N_GROUPS + 2):
+            if exists(r + 1):
+                quantise_attn(r + 1)
+            if exists(r):
+                deviation(r)
+            if exists(r + 1):
+                first_product(r + 1)
+            if exists(r + 2):
+                residual(r + 2)
+            if exists(r):
+                invert_std(r)
+            if exists(r - 1):
+                gain_and_shift(r - 1)
+            if exists(r + 2):
+                transpose_attn(r + 2)
+            if exists(r + 1):
+                finish_x(r + 1)
+            if exists(r):
+                normalise(r)
+                transpose_z(r)
+            if exists(r - 1):
+                regroup_h(r - 1)
+            if exists(r - 2):
+                finish_u(r - 2)
+            if exists(r - 1):
+                quantise_h(r - 1)
+                second_product(r - 1)
+            if exists(r + 2):
+                copy_attn(r + 2)
+            if exists(r + LOAD_AHEAD):
+                load(r + LOAD_AHEAD)

@@ -20,7 +20,7 @@ E_PASSES = E // K_PASS
 J = 2
 GROUP = J * P
 N_GROUPS = TOKENS // GROUP
-LOAD_AHEAD = 5
+LOAD_AHEAD = 8
 FLOPS = 2 * TOKENS * (E * D + D * F)
 
 
@@ -45,18 +45,17 @@ def tile_rotaryembeddingtransformerlayer_pb_t_kernel(
     with ExitStack() as ctx:
         ctx.enter_context(tc.manual_schedule())
         const = ctx.enter_context(tc.tile_pool(name="const", bufs=1))
-        loads = ctx.enter_context(tc.tile_pool(name="loads", bufs=LOAD_AHEAD))
+        loads = ctx.enter_context(tc.tile_pool(name="loads", bufs=5))
         work = ctx.enter_context(tc.tile_pool(name="work", bufs=2))
-        outs = ctx.enter_context(tc.tile_pool(name="outs", bufs=3))
-        stats = ctx.enter_context(tc.tile_pool(name="stats", bufs=3))
+        x_pool = ctx.enter_context(tc.tile_pool(name="x_pool", bufs=5))
+        u_pool = ctx.enter_context(tc.tile_pool(name="u_pool", bufs=3))
+        stats = ctx.enter_context(tc.tile_pool(name="stats", bufs=4))
         psum = ctx.enter_context(tc.psum_pool(name="psum", bufs=2))
 
         ident = const.tile([P, P], F32)
         make_identity(nc, ident[:])
         eps_col = const.tile([P, 1], F32)
         nc.vector.memset(eps_col[:], EPS)
-        table_warm = const.tile([P, 1], F32)
-        nc.scalar.activation(out=table_warm[:], in_=eps_col[:], func=ACT.Sqrt)
 
         bias_rows = const.tile([P, D + F], BF16)
         nc.vector.memset(bias_rows[:], 0.0)
@@ -70,6 +69,8 @@ def tile_rotaryembeddingtransformerlayer_pb_t_kernel(
         nc.scalar.dma_start(out=norm_rows[PACK : 2 * PACK, :], in_=be2.rearrange("(t p) -> t p", p=P))
         w1_rows = const.tile([P, F // P, D], BF16)
         nc.scalar.dma_start(out=w1_rows[:], in_=W1.rearrange("(c p) d -> p c d", p=P))
+        table_warm = const.tile([P, 1], F32)
+        nc.scalar.activation(out=table_warm[:], in_=eps_col[:], func=ACT.Sqrt)
         wo_rows = const.tile([P, D // P, E], BF16)
         wo_chunks = Wo.rearrange("(c p) k -> c p k", p=P)
         for c in range(D // P):
@@ -126,8 +127,8 @@ def tile_rotaryembeddingtransformerlayer_pb_t_kernel(
         )
 
         attn_sb, src_sb, attn_banks, attn_grouped, attn_mx = {}, {}, {}, {}, {}
-        x_sb, x_banks, neg_mean, std, inv_std, shift_z = {}, {}, {}, {}, {}, {}
-        z_sb, z_banks, h_planes, h_grouped, h_mx, u_banks = {}, {}, {}, {}, {}, {}
+        x_sb, x_banks, row_sum, neg_mean, sum_sq, std, inv_std, shift_z = {}, {}, {}, {}, {}, {}, {}, {}
+        z_sb, z_banks, h_planes, h_grouped, h_mx, u_banks, u_sb = {}, {}, {}, {}, {}, {}, {}
 
         def load(n):
             attn_tile = loads.tile([P, J, E], BF16)
@@ -162,7 +163,7 @@ def tile_rotaryembeddingtransformerlayer_pb_t_kernel(
             attn_mx[n] = (attn_codes, attn_scales)
 
         def residual(n):
-            x_tile = outs.tile([P, J, D], F32)
+            x_tile = x_pool.tile([P, J, D], F32)
             nc.vector.tensor_tensor(
                 out=x_tile[:], in0=src_sb[n][:], in1=bo_all[:].unsqueeze(1).to_broadcast([P, J, D]), op=ALU.add
             )
@@ -185,44 +186,53 @@ def tile_rotaryembeddingtransformerlayer_pb_t_kernel(
                     )
                 x_banks[n].append(x_bank)
 
-        def finish_x(n):
-            row_sum = stats.tile([P, J], F32)
-            for j in range(J):
-                nc.vector.scalar_tensor_tensor(
-                    out=x_sb[n][:, j, :],
-                    in0=x_banks[n][j][:],
-                    scalar=0.0,
-                    in1=x_sb[n][:, j, :],
-                    op0=ALU.add,
-                    op1=ALU.add,
-                    accum_out=row_sum[:, j : j + 1],
-                )
+        def finish_x(n, j):
+            if j == 0:
+                sum_tile = stats.tile([P, J], F32)
+                row_sum[n] = sum_tile
+            nc.vector.scalar_tensor_tensor(
+                out=x_sb[n][:, j, :],
+                in0=x_banks[n][j][:],
+                scalar=0.0,
+                in1=x_sb[n][:, j, :],
+                op0=ALU.add,
+                op1=ALU.add,
+                accum_out=row_sum[n][:, j : j + 1],
+            )
+
+        def mean_and_store_x(n):
             minus_mean = stats.tile([P, J], F32)
-            nc.vector.tensor_scalar_mul(out=minus_mean[:], in0=row_sum[:], scalar1=-1.0 / D)
+            nc.vector.tensor_scalar_mul(out=minus_mean[:], in0=row_sum[n][:], scalar1=-1.0 / D)
             neg_mean[n] = minus_mean
             nc.sync.dma_start(out=x_groups[n], in_=x_sb[n][:])
 
-        def deviation(n):
+        def squared_deviations(n):
             squares = work.tile([P, J, D], BF16)
-            sum_sq = stats.tile([P, J], F32)
+            sq_tile = stats.tile([P, J], F32)
             for j in range(J):
                 nc.scalar.activation(
                     out=squares[:, j, :],
                     in_=x_sb[n][:, j, :],
                     func=ACT.Square,
                     bias=neg_mean[n][:, j : j + 1],
-                    accum_out=sum_sq[:, j : j + 1],
+                    accum_out=sq_tile[:, j : j + 1],
                 )
+            sum_sq[n] = sq_tile
+
+        def standard_deviation(n):
             std_tile = stats.tile([P, J], F32)
-            nc.scalar.activation(out=std_tile[:], in_=sum_sq[:], func=ACT.Sqrt, scale=1.0 / D, bias=eps_col[:])
+            nc.scalar.activation(out=std_tile[:], in_=sum_sq[n][:], func=ACT.Sqrt, scale=1.0 / D, bias=eps_col[:])
             std[n] = std_tile
 
         def invert_std(n):
             inv_tile = stats.tile([P, J], F32)
             nc.vector.reciprocal(out=inv_tile[:], in_=std[n][:])
+            inv_std[n] = inv_tile
+
+        def shift_of_z(n):
             shift_tile = stats.tile([P, J], F32)
-            nc.vector.tensor_tensor(out=shift_tile[:], in0=neg_mean[n][:], in1=inv_tile[:], op=ALU.mult)
-            inv_std[n], shift_z[n] = inv_tile, shift_tile
+            nc.vector.tensor_tensor(out=shift_tile[:], in0=neg_mean[n][:], in1=inv_std[n][:], op=ALU.mult)
+            shift_z[n] = shift_tile
 
         def normalise(n):
             z_tile = work.tile([P, J, D], F32)
@@ -292,45 +302,59 @@ def tile_rotaryembeddingtransformerlayer_pb_t_kernel(
                 )
             u_banks[n] = u_bank
 
-        def finish_u(n):
-            u_tile = outs.tile([P, J, F], F32)
+        def add_b1(n):
+            u_tile = u_pool.tile([P, J, F], F32)
             nc.vector.tensor_tensor(
                 out=u_tile[:], in0=u_banks[n][:], in1=b1_all[:].unsqueeze(1).to_broadcast([P, J, F]), op=ALU.add
             )
-            nc.vector.tensor_scalar_max(out=u_tile[:], in0=u_tile[:], scalar1=0.0)
-            nc.sync.dma_start(out=u_groups[n], in_=u_tile[:])
+            u_sb[n] = u_tile
+
+        def relu_and_store_u(n):
+            nc.vector.tensor_scalar_max(out=u_sb[n][:], in0=u_sb[n][:], scalar1=0.0)
+            nc.sync.dma_start(out=u_groups[n], in_=u_sb[n][:])
 
         def exists(n):
             return 0 <= n < N_GROUPS
 
-        for r in range(-LOAD_AHEAD, N_GROUPS + 2):
+        for r in range(-LOAD_AHEAD, N_GROUPS + 3):
+            if exists(r + 4):
+                transpose_attn(r + 4)
+            if exists(r - 2):
+                second_product(r - 2)
             if exists(r + 1):
-                quantise_attn(r + 1)
-            if exists(r):
-                deviation(r)
-            if exists(r + 1):
-                first_product(r + 1)
+                squared_deviations(r + 1)
             if exists(r + 2):
-                residual(r + 2)
-            if exists(r):
-                invert_std(r)
+                finish_x(r + 2, 0)
+            if exists(r + 3):
+                quantise_attn(r + 3)
+            if exists(r - 3):
+                add_b1(r - 3)
+            if exists(r + 2):
+                finish_x(r + 2, 1)
+            if exists(r + 3):
+                first_product(r + 3)
             if exists(r - 1):
                 gain_and_shift(r - 1)
+            if exists(r + 4):
+                residual(r + 4)
             if exists(r + 2):
-                transpose_attn(r + 2)
+                mean_and_store_x(r + 2)
             if exists(r + 1):
-                finish_x(r + 1)
+                standard_deviation(r + 1)
+            if exists(r - 1):
+                regroup_h(r - 1)
+            if exists(r + 1):
+                invert_std(r + 1)
+            if exists(r - 3):
+                relu_and_store_u(r - 3)
             if exists(r):
                 normalise(r)
                 transpose_z(r)
             if exists(r - 1):
-                regroup_h(r - 1)
-            if exists(r - 2):
-                finish_u(r - 2)
-            if exists(r - 1):
                 quantise_h(r - 1)
-                second_product(r - 1)
-            if exists(r + 2):
-                copy_attn(r + 2)
+            if exists(r + 1):
+                shift_of_z(r + 1)
+            if exists(r + 4):
+                copy_attn(r + 4)
             if exists(r + LOAD_AHEAD):
                 load(r + LOAD_AHEAD)

@@ -21,6 +21,8 @@ J = 2
 GROUP = J * P
 N_GROUPS = TOKENS // GROUP
 LOAD_AHEAD = 8
+TR_BANKS = 4
+SECOND_LAYER_ROUND = -3
 FLOPS = 2 * TOKENS * (E * D + D * F)
 
 
@@ -80,54 +82,64 @@ def tile_rotaryembeddingtransformerlayer_pb_t_kernel(
         nc.tensor.matmul(out=bo_bank[:], lhsT=ones[:], rhs=bias_rows[:, 0:D], start=True, stop=True)
         bo_all = const.tile([P, D], F32)
         nc.vector.tensor_copy(out=bo_all[:], in_=bo_bank[:])
-        b1_bank = psum.tile([P, F], F32, tag="mm2")
-        nc.tensor.matmul(out=b1_bank[:], lhsT=ones[:], rhs=bias_rows[:, D : D + F], start=True, stop=True)
-        b1_all = const.tile([P, F], F32)
-        nc.vector.tensor_copy(out=b1_all[:], in_=b1_bank[:])
-
-        norm_rows_f32 = const.tile([P, P], F32)
-        nc.vector.tensor_copy(out=norm_rows_f32[:], in_=norm_rows[:])
-        norm_bank = psum.tile([P, P], F32, tag="z_t")
-        nc.tensor.transpose(norm_bank[:], norm_rows_f32[:], ident[:])
-        gain_shift = const.tile([P, 2 * PACK], F32)
-        nc.vector.tensor_copy(out=gain_shift[:], in_=norm_bank[:, 0 : 2 * PACK])
 
         wo_words = wo_rows[:].bitcast(F32)
         wo_grouped = const.tile([P, E_PASSES, D, PACK], BF16, align_bytes=64)
         wo_grouped_words = wo_grouped[:].bitcast(F32)
         wo_codes = const.tile([P, E_PASSES, D], U32, align_bytes=64)
         wo_scales = const.tile([P, E_PASSES, D], U8, align_bytes=64)
+
+        def quantise_wo_chunk(c):
+            rows_c = slice(c * P, (c + 1) * P)
+            for g in range(E_PASSES):
+                nc.vector.quantize_mx(
+                    out=wo_codes[:, g, rows_c].bitcast(FP8X4),
+                    scales=wo_scales[:, g, rows_c],
+                    in_=wo_grouped[:, g, rows_c, :].rearrange("p d t -> p (d t)"),
+                )
+
         for c in range(D // P):
-            wo_bank = psum.tile([P, PACK, P], F32, tag="attn_t")
+            wo_bank = psum.tile([P, PACK, P], F32, tag="tr", bufs=TR_BANKS)
             transpose_blocks(nc, wo_bank, wo_words[:, c, :], ident[:])
             copy_out = nc.vector.tensor_copy if c % 2 == 0 else nc.scalar.copy
             copy_out(out=wo_grouped_words[:, :, c * P : (c + 1) * P, :], in_=words_side_by_side(wo_bank[:]))
-        for g in range(E_PASSES):
-            nc.vector.quantize_mx(
-                out=wo_codes[:, g, :].bitcast(FP8X4),
-                scales=wo_scales[:, g, :],
-                in_=wo_grouped[:, g, :, :].rearrange("p d t -> p (d t)"),
-            )
+            if c > 0:
+                quantise_wo_chunk(c - 1)
+        quantise_wo_chunk(D // P - 1)
 
-        w1_f32 = const.tile([P, F // P, D], F32)
-        nc.vector.tensor_copy(out=w1_f32[:], in_=w1_rows[:])
-        w1_grouped = const.tile([P, F, PACK], BF16, align_bytes=64)
+        b1_all = const.tile([P, F], F32)
+        gain_shift = const.tile([P, 2 * PACK], F32)
         w1_codes = const.tile([P, F], U32, align_bytes=64)
         w1_scales = const.tile([P, F], U8, align_bytes=64)
-        for c in range(F // P):
-            w1_bank = psum.tile([P, PACK, P], F32, tag="z_t")
-            transpose_blocks(nc, w1_bank, w1_f32[:, c, :], ident[:])
-            nc.vector.tensor_copy(
-                out=w1_grouped[:, c * P : (c + 1) * P, :], in_=w1_bank[:].rearrange("p t f -> p f t")
+
+        def prepare_second_layer():
+            b1_bank = psum.tile([P, F], F32, tag="mm2")
+            nc.tensor.matmul(out=b1_bank[:], lhsT=ones[:], rhs=bias_rows[:, D : D + F], start=True, stop=True)
+            nc.vector.tensor_copy(out=b1_all[:], in_=b1_bank[:])
+
+            norm_rows_f32 = const.tile([P, P], F32)
+            nc.vector.tensor_copy(out=norm_rows_f32[:], in_=norm_rows[:])
+            norm_bank = psum.tile([P, P], F32, tag="tr", bufs=TR_BANKS)
+            nc.tensor.transpose(norm_bank[:], norm_rows_f32[:], ident[:])
+            nc.vector.tensor_copy(out=gain_shift[:], in_=norm_bank[:, 0 : 2 * PACK])
+
+            w1_f32 = const.tile([P, F // P, D], F32)
+            nc.vector.tensor_copy(out=w1_f32[:], in_=w1_rows[:])
+            w1_grouped = const.tile([P, F, PACK], BF16, align_bytes=64)
+            for c in range(F // P):
+                w1_bank = psum.tile([P, PACK, P], F32, tag="tr", bufs=TR_BANKS)
+                transpose_blocks(nc, w1_bank, w1_f32[:, c, :], ident[:])
+                nc.vector.tensor_copy(
+                    out=w1_grouped[:, c * P : (c + 1) * P, :], in_=w1_bank[:].rearrange("p t f -> p f t")
+                )
+            nc.vector.quantize_mx(
+                out=w1_codes[:].bitcast(FP8X4),
+                scales=w1_scales[:],
+                in_=w1_grouped[:].rearrange("p f t -> p (f t)"),
             )
-        nc.vector.quantize_mx(
-            out=w1_codes[:].bitcast(FP8X4),
-            scales=w1_scales[:],
-            in_=w1_grouped[:].rearrange("p f t -> p (f t)"),
-        )
 
         attn_sb, src_sb, attn_banks, attn_grouped, attn_mx = {}, {}, {}, {}, {}
-        x_sb, x_banks, row_sum, neg_mean, sum_sq, std, inv_std, shift_z = {}, {}, {}, {}, {}, {}, {}, {}
+        x_sb, x_banks, row_sum, sum_sq, std, inv_std, shift_z = {}, {}, {}, {}, {}, {}, {}
         z_sb, z_banks, h_planes, h_grouped, h_mx, u_banks, u_sb = {}, {}, {}, {}, {}, {}, {}
 
         def load(n):
@@ -141,7 +153,7 @@ def tile_rotaryembeddingtransformerlayer_pb_t_kernel(
             attn_words = attn_sb[n][:].bitcast(F32)
             attn_banks[n] = []
             for j in range(J):
-                attn_bank = psum.tile([P, PACK, P], F32, tag="attn_t")
+                attn_bank = psum.tile([P, PACK, P], F32, tag="tr", bufs=TR_BANKS)
                 transpose_blocks(nc, attn_bank, attn_words[:, j, :], ident[:])
                 attn_banks[n].append(attn_bank)
 
@@ -200,10 +212,7 @@ def tile_rotaryembeddingtransformerlayer_pb_t_kernel(
                 accum_out=row_sum[n][:, j : j + 1],
             )
 
-        def mean_and_store_x(n):
-            minus_mean = stats.tile([P, J], F32)
-            nc.vector.tensor_scalar_mul(out=minus_mean[:], in0=row_sum[n][:], scalar1=-1.0 / D)
-            neg_mean[n] = minus_mean
+        def store_x(n):
             nc.sync.dma_start(out=x_groups[n], in_=x_sb[n][:])
 
         def squared_deviations(n):
@@ -214,14 +223,15 @@ def tile_rotaryembeddingtransformerlayer_pb_t_kernel(
                     out=squares[:, j, :],
                     in_=x_sb[n][:, j, :],
                     func=ACT.Square,
-                    bias=neg_mean[n][:, j : j + 1],
+                    scale=-float(D),
+                    bias=row_sum[n][:, j : j + 1],
                     accum_out=sq_tile[:, j : j + 1],
                 )
             sum_sq[n] = sq_tile
 
         def standard_deviation(n):
             std_tile = stats.tile([P, J], F32)
-            nc.scalar.activation(out=std_tile[:], in_=sum_sq[n][:], func=ACT.Sqrt, scale=1.0 / D, bias=eps_col[:])
+            nc.scalar.activation(out=std_tile[:], in_=sum_sq[n][:], func=ACT.Sqrt, scale=1.0 / D**3, bias=eps_col[:])
             std[n] = std_tile
 
         def invert_std(n):
@@ -231,7 +241,9 @@ def tile_rotaryembeddingtransformerlayer_pb_t_kernel(
 
         def shift_of_z(n):
             shift_tile = stats.tile([P, J], F32)
-            nc.vector.tensor_tensor(out=shift_tile[:], in0=neg_mean[n][:], in1=inv_std[n][:], op=ALU.mult)
+            nc.vector.scalar_tensor_tensor(
+                out=shift_tile[:], in0=row_sum[n][:], scalar=-1.0 / D, in1=inv_std[n][:], op0=ALU.mult, op1=ALU.mult
+            )
             shift_z[n] = shift_tile
 
         def normalise(n):
@@ -249,7 +261,7 @@ def tile_rotaryembeddingtransformerlayer_pb_t_kernel(
         def transpose_z(n):
             z_banks[n] = []
             for half in range(PACK // 2):
-                z_bank = psum.tile([P, 2, GROUP], F32, tag="z_t")
+                z_bank = psum.tile([P, 2, GROUP], F32, tag="tr", bufs=TR_BANKS)
                 z_banks[n].append(z_bank)
             for j in range(J):
                 for t in range(PACK):
@@ -319,42 +331,42 @@ def tile_rotaryembeddingtransformerlayer_pb_t_kernel(
         for r in range(-LOAD_AHEAD, N_GROUPS + 3):
             if exists(r + 4):
                 transpose_attn(r + 4)
-            if exists(r - 2):
-                second_product(r - 2)
             if exists(r + 1):
                 squared_deviations(r + 1)
             if exists(r + 2):
                 finish_x(r + 2, 0)
+            if exists(r - 2):
+                quantise_h(r - 2)
+                second_product(r - 2)
             if exists(r + 3):
                 quantise_attn(r + 3)
             if exists(r - 3):
                 add_b1(r - 3)
             if exists(r + 2):
                 finish_x(r + 2, 1)
+                store_x(r + 2)
             if exists(r + 3):
                 first_product(r + 3)
-            if exists(r - 1):
-                gain_and_shift(r - 1)
-            if exists(r + 4):
-                residual(r + 4)
-            if exists(r + 2):
-                mean_and_store_x(r + 2)
-            if exists(r + 1):
-                standard_deviation(r + 1)
-            if exists(r - 1):
-                regroup_h(r - 1)
-            if exists(r + 1):
-                invert_std(r + 1)
-            if exists(r - 3):
-                relu_and_store_u(r - 3)
             if exists(r):
                 normalise(r)
-                transpose_z(r)
+            if exists(r + 4):
+                residual(r + 4)
+            if exists(r + 1):
+                standard_deviation(r + 1)
+                invert_std(r + 1)
             if exists(r - 1):
-                quantise_h(r - 1)
+                gain_and_shift(r - 1)
+            if exists(r):
+                transpose_z(r)
+            if exists(r - 3):
+                relu_and_store_u(r - 3)
             if exists(r + 1):
                 shift_of_z(r + 1)
+            if exists(r - 1):
+                regroup_h(r - 1)
             if exists(r + 4):
                 copy_attn(r + 4)
             if exists(r + LOAD_AHEAD):
                 load(r + LOAD_AHEAD)
+            if r == SECOND_LAYER_ROUND:
+                prepare_second_layer()

from contextlib import ExitStack

import concourse.mybir as mybir
from concourse.masks import make_identity

F32 = mybir.dt.float32
BF16 = mybir.dt.bfloat16
U32 = mybir.dt.uint32
U8 = mybir.dt.uint8
FP8X4 = mybir.dt.float8_e4m3fn_x4
ALU = mybir.AluOpType
ACT = mybir.ActivationFunctionType

P = 128
PACK = 4
K_PASS = P * PACK
TOKENS, E, D, F = 4096, 1024, 512, 256
EPS = 1e-5
E_PASSES = E // K_PASS
J = 2
GROUP = J * P
N_GROUPS = TOKENS // GROUP
LOAD_AHEAD = 8
TR_BANKS = 4
SECOND_LAYER_ROUND = -3
FLOPS = 2 * TOKENS * (E * D + D * F)


def transpose_blocks(nc, bank, rows, ident):
    for b in range(PACK):
        nc.tensor.transpose(bank[:, b, :], rows[:, b * P : (b + 1) * P], ident)


def words_side_by_side(bank):
    return bank.rearrange("p (g u) c -> p g c u", u=2)


def tile_rotaryembeddingtransformerlayer_pb_t_kernel(
    tc, attn, src_norm, Wo, bo, g2, be2, W1, b1, out_0, out_1
):
    nc = tc.nc
    attn_groups = attn.flatten_outer_dims().rearrange("(n p j) k -> n p j k", p=P, j=J)
    src_groups = src_norm.flatten_outer_dims().rearrange("(n p j) d -> n p j d", p=P, j=J)
    x_groups = out_0.flatten_outer_dims().rearrange("(n p j) d -> n p j d", p=P, j=J)
    u_groups = out_1.flatten_outer_dims().rearrange("(n p j) f -> n p j f", p=P, j=J)

    with ExitStack() as ctx:
        ctx.enter_context(tc.manual_schedule())
        const = ctx.enter_context(tc.tile_pool(name="const", bufs=1))
        loads = ctx.enter_context(tc.tile_pool(name="loads", bufs=5))
        work = ctx.enter_context(tc.tile_pool(name="work", bufs=2))
        x_pool = ctx.enter_context(tc.tile_pool(name="x_pool", bufs=5))
        u_pool = ctx.enter_context(tc.tile_pool(name="u_pool", bufs=3))
        stats = ctx.enter_context(tc.tile_pool(name="stats", bufs=4))
        psum = ctx.enter_context(tc.psum_pool(name="psum", bufs=2))

        ident = const.tile([P, P], F32)
        make_identity(nc, ident[:])
        eps_col = const.tile([P, 1], F32)
        nc.vector.memset(eps_col[:], EPS)

        bias_rows = const.tile([P, D + F], BF16)
        nc.vector.memset(bias_rows[:], 0.0)
        nc.scalar.dma_start(out=bias_rows[0:1, 0:D], in_=bo.rearrange("(o d) -> o d", o=1))
        nc.scalar.dma_start(out=bias_rows[0:1, D : D + F], in_=b1.rearrange("(o f) -> o f", o=1))
        ones = const.tile([P, P], BF16)
        nc.vector.memset(ones[:], 1.0)
        norm_rows = const.tile([P, P], BF16)
        nc.vector.memset(norm_rows[:], 0.0)
        nc.scalar.dma_start(out=norm_rows[0:PACK, :], in_=g2.rearrange("(t p) -> t p", p=P))
        nc.scalar.dma_start(out=norm_rows[PACK : 2 * PACK, :], in_=be2.rearrange("(t p) -> t p", p=P))
        w1_rows = const.tile([P, F // P, D], BF16)
        nc.scalar.dma_start(out=w1_rows[:], in_=W1.rearrange("(c p) d -> p c d", p=P))
        table_warm = const.tile([P, 1], F32)
        nc.scalar.activation(out=table_warm[:], in_=eps_col[:], func=ACT.Sqrt)
        wo_rows = const.tile([P, D // P, E], BF16)
        wo_chunks = Wo.rearrange("(c p) k -> c p k", p=P)
        for c in range(D // P):
            nc.sync.dma_start(out=wo_rows[:, c, :], in_=wo_chunks[c])

        bo_bank = psum.tile([P, D], F32, tag="mm1")
        nc.tensor.matmul(out=bo_bank[:], lhsT=ones[:], rhs=bias_rows[:, 0:D], start=True, stop=True)
        bo_all = const.tile([P, D], F32)
        nc.vector.tensor_copy(out=bo_all[:], in_=bo_bank[:])

        wo_words = wo_rows[:].bitcast(F32)
        wo_grouped = const.tile([P, E_PASSES, D, PACK], BF16, align_bytes=64)
        wo_grouped_words = wo_grouped[:].bitcast(F32)
        wo_codes = const.tile([P, E_PASSES, D], U32, align_bytes=64)
        wo_scales = const.tile([P, E_PASSES, D], U8, align_bytes=64)

        def quantise_wo_chunk(c):
            rows_c = slice(c * P, (c + 1) * P)
            for g in range(E_PASSES):
                nc.vector.quantize_mx(
                    out=wo_codes[:, g, rows_c].bitcast(FP8X4),
                    scales=wo_scales[:, g, rows_c],
                    in_=wo_grouped[:, g, rows_c, :].rearrange("p d t -> p (d t)"),
                )

        for c in range(D // P):
            wo_bank = psum.tile([P, PACK, P], F32, tag="tr", bufs=TR_BANKS)
            transpose_blocks(nc, wo_bank, wo_words[:, c, :], ident[:])
            copy_out = nc.vector.tensor_copy if c % 2 == 0 else nc.scalar.copy
            copy_out(out=wo_grouped_words[:, :, c * P : (c + 1) * P, :], in_=words_side_by_side(wo_bank[:]))
            if c > 0:
                quantise_wo_chunk(c - 1)
        quantise_wo_chunk(D // P - 1)

        b1_all = const.tile([P, F], F32)
        gain_shift = const.tile([P, 2 * PACK], F32)
        w1_codes = const.tile([P, F], U32, align_bytes=64)
        w1_scales = const.tile([P, F], U8, align_bytes=64)

        def prepare_second_layer():
            b1_bank = psum.tile([P, F], F32, tag="mm2")
            nc.tensor.matmul(out=b1_bank[:], lhsT=ones[:], rhs=bias_rows[:, D : D + F], start=True, stop=True)
            nc.vector.tensor_copy(out=b1_all[:], in_=b1_bank[:])

            norm_rows_f32 = const.tile([P, P], F32)
            nc.vector.tensor_copy(out=norm_rows_f32[:], in_=norm_rows[:])
            norm_bank = psum.tile([P, P], F32, tag="tr", bufs=TR_BANKS)
            nc.tensor.transpose(norm_bank[:], norm_rows_f32[:], ident[:])
            nc.vector.tensor_copy(out=gain_shift[:], in_=norm_bank[:, 0 : 2 * PACK])

            w1_f32 = const.tile([P, F // P, D], F32)
            nc.vector.tensor_copy(out=w1_f32[:], in_=w1_rows[:])
            w1_grouped = const.tile([P, F, PACK], BF16, align_bytes=64)
            for c in range(F // P):
                w1_bank = psum.tile([P, PACK, P], F32, tag="tr", bufs=TR_BANKS)
                transpose_blocks(nc, w1_bank, w1_f32[:, c, :], ident[:])
                nc.vector.tensor_copy(
                    out=w1_grouped[:, c * P : (c + 1) * P, :], in_=w1_bank[:].rearrange("p t f -> p f t")
                )
            nc.vector.quantize_mx(
                out=w1_codes[:].bitcast(FP8X4),
                scales=w1_scales[:],
                in_=w1_grouped[:].rearrange("p f t -> p (f t)"),
            )

        attn_sb, src_sb, attn_banks, attn_grouped, attn_mx = {}, {}, {}, {}, {}
        x_sb, x_banks, row_sum, sum_sq, std, inv_std, shift_z = {}, {}, {}, {}, {}, {}, {}
        z_sb, z_banks, h_planes, h_grouped, h_mx, u_banks, u_sb = {}, {}, {}, {}, {}, {}, {}

        def load(n):
            attn_tile = loads.tile([P, J, E], BF16)
            nc.sync.dma_start(out=attn_tile[:], in_=attn_groups[n])
            src_tile = loads.tile([P, J, D], BF16)
            nc.sync.dma_start(out=src_tile[:], in_=src_groups[n])
            attn_sb[n], src_sb[n] = attn_tile, src_tile

        def transpose_attn(n):
            attn_words = attn_sb[n][:].bitcast(F32)
            attn_banks[n] = []
            for j in range(J):
                attn_bank = psum.tile([P, PACK, P], F32, tag="tr", bufs=TR_BANKS)
                transpose_blocks(nc, attn_bank, attn_words[:, j, :], ident[:])
                attn_banks[n].append(attn_bank)

        def copy_attn(n):
            attn_side = work.tile([P, J, E_PASSES, P, PACK], BF16, align_bytes=64)
            attn_side_words = attn_side[:].bitcast(F32)
            for j in range(J):
                nc.scalar.copy(out=attn_side_words[:, j, :, :, :], in_=words_side_by_side(attn_banks[n][j][:]))
            attn_grouped[n] = attn_side

        def quantise_attn(n):
            attn_codes = work.tile([P, J, E_PASSES, P], U32, align_bytes=64)
            attn_scales = work.tile([P, J, E_PASSES, P], U8, align_bytes=64)
            nc.vector.quantize_mx(
                out=attn_codes[:].rearrange("p j g k -> p (j g k)").bitcast(FP8X4),
                scales=attn_scales[:].rearrange("p j g k -> p (j g k)"),
                in_=attn_grouped[n][:].rearrange("p j g k t -> p (j g k t)"),
            )
            attn_mx[n] = (attn_codes, attn_scales)

        def residual(n):
            x_tile = x_pool.tile([P, J, D], F32)
            nc.vector.tensor_tensor(
                out=x_tile[:], in0=src_sb[n][:], in1=bo_all[:].unsqueeze(1).to_broadcast([P, J, D]), op=ALU.add
            )
            x_sb[n] = x_tile

        def first_product(n):
            codes, scales = attn_mx[n]
            x_banks[n] = []
            for j in range(J):
                x_bank = psum.tile([P, D], F32, tag="mm1")
                for g in range(E_PASSES):
                    nc.tensor.matmul_mx(
                        out=x_bank[:],
                        lhsT=codes[:, j, g, :].bitcast(FP8X4),
                        lhsT_scale=scales[:, j, g, :],
                        rhs=wo_codes[:, g, :].bitcast(FP8X4),
                        rhs_scale=wo_scales[:, g, :],
                        start=(g == 0),
                        stop=(g == E_PASSES - 1),
                    )
                x_banks[n].append(x_bank)

        def finish_x(n, j):
            if j == 0:
                sum_tile = stats.tile([P, J], F32)
                row_sum[n] = sum_tile
            nc.vector.scalar_tensor_tensor(
                out=x_sb[n][:, j, :],
                in0=x_banks[n][j][:],
                scalar=0.0,
                in1=x_sb[n][:, j, :],
                op0=ALU.add,
                op1=ALU.add,
                accum_out=row_sum[n][:, j : j + 1],
            )

        def store_x(n):
            nc.sync.dma_start(out=x_groups[n], in_=x_sb[n][:])

        def squared_deviations(n):
            squares = work.tile([P, J, D], BF16)
            sq_tile = stats.tile([P, J], F32)
            for j in range(J):
                nc.scalar.activation(
                    out=squares[:, j, :],
                    in_=x_sb[n][:, j, :],
                    func=ACT.Square,
                    scale=-float(D),
                    bias=row_sum[n][:, j : j + 1],
                    accum_out=sq_tile[:, j : j + 1],
                )
            sum_sq[n] = sq_tile

        def standard_deviation(n):
            std_tile = stats.tile([P, J], F32)
            nc.scalar.activation(out=std_tile[:], in_=sum_sq[n][:], func=ACT.Sqrt, scale=1.0 / D**3, bias=eps_col[:])
            std[n] = std_tile

        def invert_std(n):
            inv_tile = stats.tile([P, J], F32)
            nc.vector.reciprocal(out=inv_tile[:], in_=std[n][:])
            inv_std[n] = inv_tile

        def shift_of_z(n):
            shift_tile = stats.tile([P, J], F32)
            nc.vector.scalar_tensor_tensor(
                out=shift_tile[:], in0=row_sum[n][:], scalar=-1.0 / D, in1=inv_std[n][:], op0=ALU.mult, op1=ALU.mult
            )
            shift_z[n] = shift_tile

        def normalise(n):
            z_tile = work.tile([P, J, D], F32)
            for j in range(J):
                nc.scalar.activation(
                    out=z_tile[:, j, :],
                    in_=x_sb[n][:, j, :],
                    func=ACT.Identity,
                    scale=inv_std[n][:, j : j + 1],
                    bias=shift_z[n][:, j : j + 1],
                )
            z_sb[n] = z_tile

        def transpose_z(n):
            z_banks[n] = []
            for half in range(PACK // 2):
                z_bank = psum.tile([P, 2, GROUP], F32, tag="tr", bufs=TR_BANKS)
                z_banks[n].append(z_bank)
            for j in range(J):
                for t in range(PACK):
                    nc.tensor.transpose(
                        z_banks[n][t // 2][:, t % 2, j * P : (j + 1) * P],
                        z_sb[n][:, j, t * P : (t + 1) * P],
                        ident[:],
                    )

        def gain_and_shift(n):
            planes = work.tile([P, PACK, GROUP], BF16)
            for t in range(PACK):
                nc.scalar.activation(
                    out=planes[:, t, :],
                    in_=z_banks[n][t // 2][:, t % 2, :],
                    func=ACT.Identity,
                    scale=gain_shift[:, t : t + 1],
                    bias=gain_shift[:, PACK + t : PACK + t + 1],
                )
            h_planes[n] = planes

        def regroup_h(n):
            h_side = work.tile([P, GROUP, PACK], BF16, align_bytes=64)
            nc.vector.tensor_copy(
                out=h_side[:].rearrange("p (c i) t -> p c t i", i=4),
                in_=h_planes[n][:].rearrange("p t (c i) -> p c t i", i=4),
            )
            h_grouped[n] = h_side

        def quantise_h(n):
            h_codes = work.tile([P, GROUP], U32, align_bytes=64)
            h_scales = work.tile([P, GROUP], U8, align_bytes=64)
            nc.vector.quantize_mx(
                out=h_codes[:].bitcast(FP8X4), scales=h_scales[:], in_=h_grouped[n][:].rearrange("p k t -> p (k t)")
            )
            h_mx[n] = (h_codes, h_scales)

        def second_product(n):
            codes, scales = h_mx[n]
            u_bank = psum.tile([P, J, F], F32, tag="mm2")
            for j in range(J):
                nc.tensor.matmul_mx(
                    out=u_bank[:, j, :],
                    lhsT=codes[:, j * P : (j + 1) * P].bitcast(FP8X4),
                    lhsT_scale=scales[:, j * P : (j + 1) * P],
                    rhs=w1_codes[:].bitcast(FP8X4),
                    rhs_scale=w1_scales[:],
                    start=True,
                    stop=True,
                )
            u_banks[n] = u_bank

        def add_b1(n):
            u_tile = u_pool.tile([P, J, F], F32)
            nc.vector.tensor_tensor(
                out=u_tile[:], in0=u_banks[n][:], in1=b1_all[:].unsqueeze(1).to_broadcast([P, J, F]), op=ALU.add
            )
            u_sb[n] = u_tile

        def relu_and_store_u(n):
            nc.vector.tensor_scalar_max(out=u_sb[n][:], in0=u_sb[n][:], scalar1=0.0)
            nc.sync.dma_start(out=u_groups[n], in_=u_sb[n][:])

        def exists(n):
            return 0 <= n < N_GROUPS

        for r in range(-LOAD_AHEAD, N_GROUPS + 3):
            if exists(r + 4):
                transpose_attn(r + 4)
            if exists(r + 1):
                squared_deviations(r + 1)
            if exists(r + 2):
                finish_x(r + 2, 0)
            if exists(r - 2):
                quantise_h(r - 2)
                second_product(r - 2)
            if exists(r + 3):
                quantise_attn(r + 3)
            if exists(r - 3):
                add_b1(r - 3)
            if exists(r + 2):
                finish_x(r + 2, 1)
                store_x(r + 2)
            if exists(r + 3):
                first_product(r + 3)
            if exists(r):
                normalise(r)
            if exists(r + 4):
                residual(r + 4)
            if exists(r + 1):
                standard_deviation(r + 1)
                invert_std(r + 1)
            if exists(r - 1):
                gain_and_shift(r - 1)
            if exists(r):
                transpose_z(r)
            if exists(r - 3):
                relu_and_store_u(r - 3)
            if exists(r + 1):
                shift_of_z(r + 1)
            if exists(r - 1):
                regroup_h(r - 1)
            if exists(r + 4):
                copy_attn(r + 4)
            if exists(r + LOAD_AHEAD):
                load(r + LOAD_AHEAD)
            if r == SECOND_LAYER_ROUND:
                prepare_second_layer()
